import numpy as np
import ml_dtypes


def mxq(x, axis, fmt="e4m3"):
    dtype, down = {"e4m3": (ml_dtypes.float8_e4m3fn, 7), "e5m2": (ml_dtypes.float8_e5m2, 14)}[fmt]
    v = np.moveaxis(np.asarray(x, np.float32).astype(ml_dtypes.bfloat16).astype(np.float64), axis, -1)
    blocks = v.reshape(v.shape[:-1] + (-1, 32))
    amax = np.abs(blocks).max(-1, keepdims=True)
    byte = np.maximum(np.where(amax > 0, np.frexp(amax)[1] - 1 + 127, 0) - down, 1)
    scale = np.exp2(byte - 127.0)
    codes = (blocks / scale).astype(np.float32).astype(dtype).astype(np.float64)
    return np.moveaxis((codes * scale).reshape(v.shape), -1, axis)


WIDE = False


def mx_kscale(k):
    if not WIDE:
        return np.ones(k)
    levels = np.array([10, -10, 5, -5, 0])
    a = np.random.permutation(np.resize(levels, k // 512 * 4)).reshape(k // 512, 4)
    idx = np.arange(k)
    return np.exp2(a[idx // 512, idx % 128 // 32])


BF16 = ml_dtypes.bfloat16


def bf(x):
    return np.asarray(x, np.float32).astype(BF16)


def f64(x):
    return np.asarray(x).astype(np.float64)


B, D_W, D_C, D_P, R = 4096, 512, 512, 512, 512
D_X = D_C + D_P


def setup_inputs():
    s = mx_kscale(D_X)
    t = mx_kscale(R)
    return {
        "w_prev": bf(np.random.standard_normal((B, D_W))),
        "z_t": bf(np.random.standard_normal((B, D_P)) * s[D_C:]),
        "c_t": bf(np.random.standard_normal((B, D_C)) * s[:D_C]),
        "A_diag": bf(np.random.standard_normal(D_W) * 0.7),
        "A_U": bf(np.random.standard_normal((D_W, R)) / np.sqrt(R) / t),
        "A_V": bf(np.random.standard_normal((D_W, R)) / np.sqrt(D_W) * t),
        "W_mod": bf(np.random.standard_normal((D_C, D_W)) / np.sqrt(D_C) / s[:D_C, None]),
        "b_mod": bf(np.random.standard_normal(D_W) * 0.3),
        "W_B": bf(np.random.standard_normal((D_X, D_W)) / np.sqrt(D_X) / s[:, None]),
        "b_B": bf(np.random.standard_normal(D_W) * 0.3),
    }


def reference(w_prev, z_t, c_t, A_diag, A_U, A_V, W_mod, b_mod, W_B, b_B):
    w = f64(w_prev)
    a_diag = np.tanh(f64(A_diag)) * 0.9
    xq = mxq(np.concatenate([f64(c_t), f64(z_t)], axis=-1), 1, "e4m3")
    modulation = np.tanh((xq[:, :D_C] @ mxq(f64(W_mod), 0, "e4m3")) + f64(b_mod))
    h = mxq(w, 1, "e4m3") @ mxq(f64(A_V), 0, "e4m3")
    Aw = a_diag * w + (mxq(h, 1, "e4m3") @ mxq(f64(A_U), 1, "e4m3").T)
    Bt = (xq @ mxq(f64(W_B), 0, "e4m3")) + f64(b_B)
    return modulation * Aw + Bt

@@ -1,0 +1,309 @@
+from contextlib import ExitStack
+
+import concourse.mybir as mybir
+from concourse.masks import make_identity
+
+F32 = mybir.dt.float32
+BF16 = mybir.dt.bfloat16
+U32 = mybir.dt.uint32
+U8 = mybir.dt.uint8
+FP8X4 = mybir.dt.float8_e4m3fn_x4
+ALU = mybir.AluOpType
+ACT = mybir.ActivationFunctionType
+
+P = 128
+PACK = 4
+WIDTH = P * PACK
+CHUNKS = WIDTH // P
+ROWS = 4096
+SLAB = 256
+N_SLABS = ROWS // SLAB
+PAIR = 2 * SLAB
+ROW_BUFS = 6
+AHEAD = 2
+OUT_LAG = 3
+
+FLOPS = 2 * ROWS * WIDTH * 5 * WIDTH
+
+
+def tile_wavesubsystem_pa_t_kernel(
+    tc, w_prev, z_t, c_t, A_diag, A_U, A_V, W_mod, b_mod, W_B, b_B, out
+):
+    nc = tc.nc
+    activations = {"w": w_prev, "c": c_t, "z": z_t}
+    k_first_weights = {
+        "A_V": A_V,
+        "W_mod": W_mod,
+        "W_B_c": W_B[0:WIDTH, :],
+        "W_B_z": W_B[WIDTH : 2 * WIDTH, :],
+    }
+
+    with ExitStack() as ctx:
+        consts = ctx.enter_context(tc.tile_pool(name="consts", bufs=1))
+        rows_pool = ctx.enter_context(tc.tile_pool(name="rows", bufs=ROW_BUFS))
+        grouped_pool = ctx.enter_context(tc.tile_pool(name="grouped", bufs=3))
+        codes_pool = ctx.enter_context(tc.tile_pool(name="codes", bufs=3))
+        work = ctx.enter_context(tc.tile_pool(name="work", bufs=3))
+        psum = ctx.enter_context(tc.psum_pool(name="psum", bufs=8))
+        ctx.enter_context(tc.manual_schedule())
+
+        def new_bank():
+            return psum.tile([P, WIDTH], F32, name="bank", tag="bank")
+
+        rows = {}
+        grouped = {}
+        codes = {}
+        scales = {}
+        raw = {}
+        gated = {}
+        out_t = {}
+
+        def new_mx_operand(key, name):
+            codes[key] = codes_pool.tile([P, WIDTH], U32, name=name + "_codes", align_bytes=64)
+            scales[key] = codes_pool.tile([P, WIDTH], U8, name=name + "_scales", align_bytes=64)
+
+        def quantise(source, key, first, count):
+            nc.vector.quantize_mx(
+                out=codes[key][:, first : first + count].bitcast(FP8X4),
+                scales=scales[key][:, first : first + count],
+                in_=source[:, PACK * first : PACK * (first + count)],
+            )
+
+        def multiply(acc, weight, chunk, moving, cols, start=True, stop=True):
+            features = slice(chunk * P, (chunk + 1) * P)
+            nc.tensor.matmul_mx(
+                out=acc,
+                lhsT=codes[weight][:, features].bitcast(FP8X4),
+                lhsT_scale=scales[weight][:, features],
+                rhs=codes[moving][:, cols].bitcast(FP8X4),
+                rhs_scale=scales[moving][:, cols],
+                start=start,
+                stop=stop,
+            )
+
+
+        def load_rows(tile, source, slab):
+            nc.sync.dma_start(
+                out=tile[:],
+                in_=source[slab * SLAB : (slab + 1) * SLAB, :].rearrange("(q e) k -> q (e k)", e=2),
+            )
+
+        def load_slab(slab):
+            for name in ("w", "c", "z"):
+                rows[(name, slab)] = rows_pool.tile([P, 2 * WIDTH], BF16, name="rows_" + name)
+                load_rows(rows[(name, slab)], activations[name], slab)
+
+        def load_k_first_weight(name):
+            raw[name] = consts.tile([P, PACK * WIDTH], BF16, name="raw_" + name)
+            nc.sync.dma_start(
+                out=raw[name][:].rearrange("i (u x) -> i u x", u=2),
+                in_=k_first_weights[name].rearrange("(u i e) n -> i u (e n)", u=2, e=2),
+            )
+
+
+        def transpose_slab(tile, target, half):
+            words = tile[:].bitcast(F32).rearrange("q (e u i) -> q e u i", e=2, u=2)
+            bank = new_bank()
+            planes = bank[:].rearrange("i (u e q) -> i u e q", u=2, e=2)
+            for e in range(2):
+                for u in range(2):
+                    nc.tensor.transpose(planes[:, u, e, :], words[:, e, u, :], identity[:])
+            pairs = target[:].bitcast(F32).rearrange("i (col u) -> i col u", u=2)
+            nc.scalar.copy(
+                out=pairs[:, half * SLAB : (half + 1) * SLAB, :],
+                in_=bank[:].rearrange("i (u col) -> i col u", u=2),
+            )
+
+        def transpose_in(slab):
+            pair, half = divmod(slab, 2)
+            for name in ("w", "c", "z"):
+                if half == 0:
+                    grouped[(name, pair)] = grouped_pool.tile(
+                        [P, PACK * PAIR], BF16, name="grouped_" + name, align_bytes=64
+                    )
+                    new_mx_operand((name, pair), name)
+                transpose_slab(rows[(name, slab)], grouped[(name, pair)], half)
+            if slab + ROW_BUFS < N_SLABS:
+                load_slab(slab + ROW_BUFS)
+
+        def quantise_slab(name, slab):
+            pair, half = divmod(slab, 2)
+            quantise(grouped[(name, pair)], (name, pair), half * SLAB, SLAB)
+
+
+        def quantise_k_first_weight(name):
+            source = raw[name][:].rearrange("i (t u q e) -> i t u e q", t=PACK, u=2, e=2)
+            staged = grouped_pool.tile([P, PACK * WIDTH], BF16, name="grouped_weight", align_bytes=64)
+            target = staged[:].rearrange("i (c q t) -> i c q t", c=CHUNKS, t=PACK)
+            for chunk in range(CHUNKS):
+                u, e = divmod(chunk, 2)
+                copy = nc.vector.tensor_copy if chunk % 2 == 0 else nc.scalar.copy
+                copy(out=target[:, chunk], in_=source[:, :, u, e, :].rearrange("i t q -> i q t"))
+            new_weight_operand(name)
+            quantise(staged, name, 0, WIDTH)
+
+        def new_weight_operand(name):
+            codes[name] = consts.tile([P, WIDTH], U32, name=name + "_codes", align_bytes=64)
+            scales[name] = consts.tile([P, WIDTH], U8, name=name + "_scales", align_bytes=64)
+
+        def quantise_a_u():
+            staged = grouped_pool.tile([P, PACK * WIDTH], BF16, name="grouped_weight", align_bytes=64)
+            for half in range(2):
+                transpose_slab(rows[("A_U", half)], staged, half)
+            new_weight_operand("A_U")
+            quantise(staged, "A_U", 0, WIDTH)
+
+        def spread_vectors():
+            bank = new_bank()
+            nc.tensor.transpose(bank[:, 0:P], vector_rows[:].bitcast(F32), identity[:])
+            words = consts.tile([P, 8], F32, name="vector_words")
+            nc.vector.tensor_copy(out=words[:], in_=bank[:, 0:8])
+            nc.vector.tensor_copy(out=vector_cols[:], in_=words[:].bitcast(BF16))
+            nc.scalar.activation(out=a_cols[:], in_=vector_cols[:, 8:12], func=ACT.Tanh)
+            nc.vector.tensor_scalar_mul(out=a_cols[:], in0=a_cols[:], scalar1=0.9)
+
+
+        def hidden(slab):
+            pair, half = divmod(slab, 2)
+            if half == 0:
+                grouped[("h", pair)] = grouped_pool.tile(
+                    [P, PACK * PAIR], BF16, name="grouped_h", align_bytes=64
+                )
+                new_mx_operand(("h", pair), "h")
+            target = grouped[("h", pair)][:].rearrange("i (col t) -> i col t", t=PACK)
+            for e in range(2):
+                cols = slice(half * SLAB + e * P, half * SLAB + (e + 1) * P)
+                bank = new_bank()
+                parts = bank[:].rearrange("i (t q) -> i t q", t=PACK)
+                for t in range(PACK):
+                    multiply(parts[:, t, :], "A_V", t, ("w", pair), cols)
+                copy = nc.scalar.copy if e == 0 else nc.vector.tensor_copy
+                copy(out=target[:, cols, :], in_=parts.rearrange("i t q -> i q t"))
+
+
+        def gate_and_state(pair, chunk):
+            everything = slice(0, PAIR)
+            gate_bank = new_bank()
+            multiply(gate_bank[:], "W_mod", chunk, ("c", pair), everything)
+            gate = work.tile([P, PAIR], F32, name="gate")
+            nc.scalar.activation(
+                out=gate[:], in_=gate_bank[:], func=ACT.Tanh, bias=vector_cols[:, chunk : chunk + 1]
+            )
+            state_bank = new_bank()
+            multiply(state_bank[:], "A_U", chunk, ("h", pair), everything)
+            state = work.tile([P, PAIR], F32, name="state")
+            w_t = grouped[("w", pair)][:].rearrange("i (col t) -> i col t", t=PACK)[:, :, chunk]
+            nc.vector.scalar_tensor_tensor(
+                out=state[:],
+                in0=w_t,
+                scalar=a_cols[:, chunk : chunk + 1],
+                in1=state_bank[:],
+                op0=ALU.mult,
+                op1=ALU.add,
+            )
+            gated[chunk] = work.tile([P, PAIR], F32, name="gated")
+            nc.gpsimd.tensor_tensor(out=gated[chunk][:], in0=gate[:], in1=state[:], op=ALU.mult)
+
+        def drive_and_sum(pair, chunk):
+            everything = slice(0, PAIR)
+            drive_bank = new_bank()
+            multiply(drive_bank[:], "W_B_c", chunk, ("c", pair), everything, start=True, stop=False)
+            multiply(drive_bank[:], "W_B_z", chunk, ("z", pair), everything, start=False, stop=True)
+            nc.vector.scalar_tensor_tensor(
+                out=out_t[pair][:, chunk, :],
+                in0=drive_bank[:],
+                scalar=vector_cols[:, PACK + chunk : PACK + chunk + 1],
+                in1=gated[chunk][:],
+                op0=ALU.add,
+                op1=ALU.add,
+            )
+
+
+        def transpose_out(slab):
+            pair, half = divmod(slab, 2)
+            result = work.tile([P, 2 * WIDTH], F32, name="result")
+            for e in range(2):
+                cols = slice(half * SLAB + e * P, half * SLAB + (e + 1) * P)
+                bank = new_bank()
+                parts = bank[:].rearrange("q (t i) -> q t i", t=CHUNKS)
+                for chunk in range(CHUNKS):
+                    nc.tensor.transpose(parts[:, chunk, :], out_t[pair][:, chunk, cols], identity[:])
+                nc.scalar.copy(
+                    out=result[:, e * WIDTH : (e + 1) * WIDTH].rearrange(
+                        "q (u i e2) -> q u i e2", u=2, e2=2
+                    ),
+                    in_=bank[:].rearrange("q (u e2 i) -> q u i e2", u=2, e2=2),
+                )
+            nc.sync.dma_start(
+                out=out[slab * SLAB : (slab + 1) * SLAB, :].rearrange("(q e) d -> q (e d)", e=2),
+                in_=result[:],
+            )
+
+
+        identity = consts.tile([P, P], F32, name="identity")
+        make_identity(nc, identity[:])
+        vector_rows = consts.tile([P, 2 * P], BF16, name="vector_rows")
+        vector_cols = consts.tile([P, 16], F32, name="vector_cols")
+        a_cols = consts.tile([P, CHUNKS], F32, name="a_cols")
+        nc.vector.memset(vector_rows[:], 0.0)
+        for v, vector in enumerate((b_mod, b_B, A_diag)):
+            nc.scalar.dma_start(
+                out=vector_rows[2 * v : 2 * v + 2, :], in_=vector.rearrange("(u x) -> u x", u=2)
+            )
+
+        load_slab(0)
+        load_k_first_weight("A_V")
+        load_slab(1)
+        for half in range(2):
+            rows[("A_U", half)] = consts.tile([P, 2 * WIDTH], BF16, name="rows_A_U_%d" % half)
+            load_rows(rows[("A_U", half)], A_U, half)
+        load_k_first_weight("W_mod")
+        load_slab(2)
+        load_k_first_weight("W_B_c")
+        load_k_first_weight("W_B_z")
+        for slab in range(3, ROW_BUFS):
+            load_slab(slab)
+
+        transpose_in(0)
+        quantise_k_first_weight("A_V")
+        for name in ("w", "c", "z"):
+            quantise_slab(name, 0)
+        hidden(0)
+        transpose_in(1)
+        quantise_a_u()
+        spread_vectors()
+        for name in ("w", "c", "z"):
+            quantise_slab(name, 1)
+        hidden(1)
+        quantise_slab("h", 0)
+        quantise_k_first_weight("W_mod")
+        quantise_slab("h", 1)
+        quantise_k_first_weight("W_B_c")
+        quantise_k_first_weight("W_B_z")
+
+        for step in range(N_SLABS + OUT_LAG):
+            pair, half = divmod(step, 2)
+            coming = step + AHEAD
+            leaving = step - OUT_LAG
+            chunks = (2 * half, 2 * half + 1)
+            if coming < N_SLABS:
+                transpose_in(coming)
+            if leaving >= 0:
+                transpose_out(leaving)
+            if coming < N_SLABS:
+                quantise_slab("w", coming)
+            if step < N_SLABS:
+                if half == 0:
+                    out_t[pair] = work.tile([P, CHUNKS, PAIR], F32, name="out_t")
+                for chunk in chunks:
+                    gate_and_state(pair, chunk)
+            if coming < N_SLABS:
+                hidden(coming)
+                quantise_slab("c", coming)
+                quantise_slab("z", coming)
+            if step < N_SLABS:
+                drive_and_sum(pair, chunks[0])
+            if coming < N_SLABS:
+                quantise_slab("h", coming)
+            if step < N_SLABS:
+                drive_and_sum(pair, chunks[1])

@@ -20,7 +20,8 @@ SLAB = 256
 N_SLABS = ROWS // SLAB
 PAIR = 2 * SLAB
 ROW_BUFS = 6
-AHEAD = 2
+IN_LEAD = 3
+HIDDEN_LEAD = 2
 OUT_LAG = 3
 
 FLOPS = 2 * ROWS * WIDTH * 5 * WIDTH
@@ -55,6 +56,8 @@ def tile_wavesubsystem_pa_t_kernel(
         codes = {}
         scales = {}
         raw = {}
+        gates = {}
+        states = {}
         gated = {}
         out_t = {}
 
@@ -181,31 +184,38 @@ def tile_wavesubsystem_pa_t_kernel(
                 copy(out=target[:, cols, :], in_=parts.rearrange("i t q -> i q t"))
 
 
-        def gate_and_state(pair, chunk):
-            everything = slice(0, PAIR)
+        everything = slice(0, PAIR)
+
+        def gate(pair, chunk):
             gate_bank = new_bank()
             multiply(gate_bank[:], "W_mod", chunk, ("c", pair), everything)
-            gate = work.tile([P, PAIR], F32, name="gate")
+            gates[chunk] = work.tile([P, PAIR], F32, name="gate")
             nc.scalar.activation(
-                out=gate[:], in_=gate_bank[:], func=ACT.Tanh, bias=vector_cols[:, chunk : chunk + 1]
+                out=gates[chunk][:], in_=gate_bank[:], func=ACT.Tanh, bias=vector_cols[:, chunk : chunk + 1]
             )
+
+        def state(pair, chunk):
             state_bank = new_bank()
             multiply(state_bank[:], "A_U", chunk, ("h", pair), everything)
-            state = work.tile([P, PAIR], F32, name="state")
+            states[chunk] = work.tile([P, PAIR], F32, name="state")
             w_t = grouped[("w", pair)][:].rearrange("i (col t) -> i col t", t=PACK)[:, :, chunk]
             nc.vector.scalar_tensor_tensor(
-                out=state[:],
+                out=states[chunk][:],
                 in0=w_t,
                 scalar=a_cols[:, chunk : chunk + 1],
                 in1=state_bank[:],
                 op0=ALU.mult,
                 op1=ALU.add,
             )
+
+        def gate_the_state(chunk):
             gated[chunk] = work.tile([P, PAIR], F32, name="gated")
-            nc.gpsimd.tensor_tensor(out=gated[chunk][:], in0=gate[:], in1=state[:], op=ALU.mult)
+            engine = nc.gpsimd if chunk % 2 == 0 else nc.vector
+            engine.tensor_tensor(
+                out=gated[chunk][:], in0=gates[chunk][:], in1=states[chunk][:], op=ALU.mult
+            )
 
         def drive_and_sum(pair, chunk):
-            everything = slice(0, PAIR)
             drive_bank = new_bank()
             multiply(drive_bank[:], "W_B_c", chunk, ("c", pair), everything, start=True, stop=False)
             multiply(drive_bank[:], "W_B_z", chunk, ("z", pair), everything, start=False, stop=True)
@@ -268,42 +278,49 @@ def tile_wavesubsystem_pa_t_kernel(
         quantise_k_first_weight("A_V")
         for name in ("w", "c", "z"):
             quantise_slab(name, 0)
-        hidden(0)
         transpose_in(1)
-        quantise_a_u()
-        spread_vectors()
+        hidden(0)
         for name in ("w", "c", "z"):
             quantise_slab(name, 1)
+        quantise_a_u()
+        spread_vectors()
         hidden(1)
         quantise_slab("h", 0)
         quantise_k_first_weight("W_mod")
         quantise_slab("h", 1)
+        transpose_in(2)
         quantise_k_first_weight("W_B_c")
         quantise_k_first_weight("W_B_z")
 
         for step in range(N_SLABS + OUT_LAG):
             pair, half = divmod(step, 2)
-            coming = step + AHEAD
-            leaving = step - OUT_LAG
-            chunks = (2 * half, 2 * half + 1)
-            if coming < N_SLABS:
-                transpose_in(coming)
-            if leaving >= 0:
-                transpose_out(leaving)
-            if coming < N_SLABS:
-                quantise_slab("w", coming)
-            if step < N_SLABS:
-                if half == 0:
-                    out_t[pair] = work.tile([P, CHUNKS, PAIR], F32, name="out_t")
-                for chunk in chunks:
-                    gate_and_state(pair, chunk)
-            if coming < N_SLABS:
-                hidden(coming)
-                quantise_slab("c", coming)
-                quantise_slab("z", coming)
-            if step < N_SLABS:
-                drive_and_sum(pair, chunks[0])
-            if coming < N_SLABS:
-                quantise_slab("h", coming)
-            if step < N_SLABS:
-                drive_and_sum(pair, chunks[1])
+            chunk = 2 * half
+            last_pair, last_half = divmod(step - 1, 2)
+            last_chunk = 2 * last_half
+            working = step < N_SLABS
+            summing = 0 < step <= N_SLABS
+            if step + IN_LEAD < N_SLABS:
+                transpose_in(step + IN_LEAD)
+            if step >= OUT_LAG:
+                transpose_out(step - OUT_LAG)
+            if step + HIDDEN_LEAD < N_SLABS:
+                for name in ("w", "c", "z"):
+                    quantise_slab(name, step + HIDDEN_LEAD)
+            if 0 < step and step - 1 + HIDDEN_LEAD < N_SLABS:
+                quantise_slab("h", step - 1 + HIDDEN_LEAD)
+            if summing:
+                gate_the_state(last_chunk + 1)
+                if last_half == 0:
+                    out_t[last_pair] = work.tile([P, CHUNKS, PAIR], F32, name="out_t")
+            if working:
+                gate(pair, chunk)
+                state(pair, chunk)
+                gate(pair, chunk + 1)
+                state(pair, chunk + 1)
+            if step + HIDDEN_LEAD < N_SLABS:
+                hidden(step + HIDDEN_LEAD)
+            if summing:
+                drive_and_sum(last_pair, last_chunk)
+                drive_and_sum(last_pair, last_chunk + 1)
+            if working:
+                gate_the_state(chunk)

@@ -43,8 +43,9 @@ def tile_wavesubsystem_pa_t_kernel(
         consts = ctx.enter_context(tc.tile_pool(name="consts", bufs=1))
         rows_pool = ctx.enter_context(tc.tile_pool(name="rows", bufs=ROW_BUFS))
         grouped_pool = ctx.enter_context(tc.tile_pool(name="grouped", bufs=3))
+        staging = ctx.enter_context(tc.tile_pool(name="staging", bufs=3))
         codes_pool = ctx.enter_context(tc.tile_pool(name="codes", bufs=3))
-        work = ctx.enter_context(tc.tile_pool(name="work", bufs=3))
+        work = ctx.enter_context(tc.tile_pool(name="work", bufs=4))
         psum = ctx.enter_context(tc.psum_pool(name="psum", bufs=8))
         ctx.enter_context(tc.manual_schedule())
 
@@ -55,10 +56,12 @@ def tile_wavesubsystem_pa_t_kernel(
         grouped = {}
         codes = {}
         scales = {}
+        staged = {}
         raw = {}
         gates = {}
         states = {}
         gated = {}
+        results = {}
         out_t = {}
 
         def new_mx_operand(key, name):
@@ -91,8 +94,8 @@ def tile_wavesubsystem_pa_t_kernel(
                 in_=source[slab * SLAB : (slab + 1) * SLAB, :].rearrange("(q e) k -> q (e k)", e=2),
             )
 
-        def load_slab(slab):
-            for name in ("w", "c", "z"):
+        def load_slab(slab, names=("w", "c", "z")):
+            for name in names:
                 rows[(name, slab)] = rows_pool.tile([P, 2 * WIDTH], BF16, name="rows_" + name)
                 load_rows(rows[(name, slab)], activations[name], slab)
 
@@ -104,7 +107,7 @@ def tile_wavesubsystem_pa_t_kernel(
             )
 
 
-        def transpose_slab(tile, target, half):
+        def transpose_slab(tile, target, half, copy=nc.scalar.copy):
             words = tile[:].bitcast(F32).rearrange("q (e u i) -> q e u i", e=2, u=2)
             bank = new_bank()
             planes = bank[:].rearrange("i (u e q) -> i u e q", u=2, e=2)
@@ -112,49 +115,51 @@ def tile_wavesubsystem_pa_t_kernel(
                 for u in range(2):
                     nc.tensor.transpose(planes[:, u, e, :], words[:, e, u, :], identity[:])
             pairs = target[:].bitcast(F32).rearrange("i (col u) -> i col u", u=2)
-            nc.scalar.copy(
+            copy(
                 out=pairs[:, half * SLAB : (half + 1) * SLAB, :],
                 in_=bank[:].rearrange("i (u col) -> i col u", u=2),
             )
 
-        def transpose_in(slab):
+        def transpose_in(slab, names=("w", "c", "z"), copy=nc.scalar.copy):
             pair, half = divmod(slab, 2)
-            for name in ("w", "c", "z"):
-                if half == 0:
+            for name in names:
+                if (name, pair) not in grouped:
                     grouped[(name, pair)] = grouped_pool.tile(
                         [P, PACK * PAIR], BF16, name="grouped_" + name, align_bytes=64
                     )
                     new_mx_operand((name, pair), name)
-                transpose_slab(rows[(name, slab)], grouped[(name, pair)], half)
-            if slab + ROW_BUFS < N_SLABS:
+                transpose_slab(rows[(name, slab)], grouped[(name, pair)], half, copy)
+            if "z" in names and slab + ROW_BUFS < N_SLABS:
                 load_slab(slab + ROW_BUFS)
+
+        def quantise_pair(name, pair):
+            quantise(grouped[(name, pair)], (name, pair), 0, PAIR)
 
         def quantise_slab(name, slab):
             pair, half = divmod(slab, 2)
             quantise(grouped[(name, pair)], (name, pair), half * SLAB, SLAB)
 
 
-        def quantise_k_first_weight(name):
+        def stage_chunk(name, chunk, copy):
             source = raw[name][:].rearrange("i (t u q e) -> i t u e q", t=PACK, u=2, e=2)
-            staged = grouped_pool.tile([P, PACK * WIDTH], BF16, name="grouped_weight", align_bytes=64)
-            target = staged[:].rearrange("i (c q t) -> i c q t", c=CHUNKS, t=PACK)
-            for chunk in range(CHUNKS):
-                u, e = divmod(chunk, 2)
-                copy = nc.vector.tensor_copy if chunk % 2 == 0 else nc.scalar.copy
-                copy(out=target[:, chunk], in_=source[:, :, u, e, :].rearrange("i t q -> i q t"))
+            if name not in staged:
+                staged[name] = staging.tile([P, PACK * WIDTH], BF16, name="staged", align_bytes=64)
+            target = staged[name][:].rearrange("i (c q t) -> i c q t", c=CHUNKS, t=PACK)
+            u, e = divmod(chunk, 2)
+            copy(out=target[:, chunk], in_=source[:, :, u, e, :].rearrange("i t q -> i q t"))
+
+        def quantise_weight(name):
             new_weight_operand(name)
-            quantise(staged, name, 0, WIDTH)
+            quantise(staged[name], name, 0, WIDTH)
 
         def new_weight_operand(name):
             codes[name] = consts.tile([P, WIDTH], U32, name=name + "_codes", align_bytes=64)
             scales[name] = consts.tile([P, WIDTH], U8, name=name + "_scales", align_bytes=64)
 
-        def quantise_a_u():
-            staged = grouped_pool.tile([P, PACK * WIDTH], BF16, name="grouped_weight", align_bytes=64)
-            for half in range(2):
-                transpose_slab(rows[("A_U", half)], staged, half)
-            new_weight_operand("A_U")
-            quantise(staged, "A_U", 0, WIDTH)
+        def stage_a_u(half, copy=nc.scalar.copy):
+            if "A_U" not in staged:
+                staged["A_U"] = staging.tile([P, PACK * WIDTH], BF16, name="staged", align_bytes=64)
+            transpose_slab(rows[("A_U", half)], staged["A_U"], half, copy)
 
         def spread_vectors():
             bank = new_bank()
@@ -166,22 +171,20 @@ def tile_wavesubsystem_pa_t_kernel(
             nc.vector.tensor_scalar_mul(out=a_cols[:], in0=a_cols[:], scalar1=0.9)
 
 
-        def hidden(slab):
+        def hidden(slab, e, copy):
             pair, half = divmod(slab, 2)
-            if half == 0:
+            if ("h", pair) not in grouped:
                 grouped[("h", pair)] = grouped_pool.tile(
                     [P, PACK * PAIR], BF16, name="grouped_h", align_bytes=64
                 )
                 new_mx_operand(("h", pair), "h")
             target = grouped[("h", pair)][:].rearrange("i (col t) -> i col t", t=PACK)
-            for e in range(2):
-                cols = slice(half * SLAB + e * P, half * SLAB + (e + 1) * P)
-                bank = new_bank()
-                parts = bank[:].rearrange("i (t q) -> i t q", t=PACK)
-                for t in range(PACK):
-                    multiply(parts[:, t, :], "A_V", t, ("w", pair), cols)
-                copy = nc.scalar.copy if e == 0 else nc.vector.tensor_copy
-                copy(out=target[:, cols, :], in_=parts.rearrange("i t q -> i q t"))
+            cols = slice(half * SLAB + e * P, half * SLAB + (e + 1) * P)
+            bank = new_bank()
+            parts = bank[:].rearrange("i (t q) -> i t q", t=PACK)
+            for t in range(PACK):
+                multiply(parts[:, t, :], "A_V", t, ("w", pair), cols)
+            copy(out=target[:, cols, :], in_=parts.rearrange("i t q -> i q t"))
 
 
         everything = slice(0, PAIR)
@@ -208,46 +211,49 @@ def tile_wavesubsystem_pa_t_kernel(
                 op1=ALU.add,
             )
 
-        def gate_the_state(chunk):
-            gated[chunk] = work.tile([P, PAIR], F32, name="gated")
-            engine = nc.gpsimd if chunk % 2 == 0 else nc.vector
+        def gate_the_state(pair, chunk, engine=nc.gpsimd):
+            gated[(pair, chunk)] = work.tile([P, PAIR], F32, name="gated", bufs=6)
             engine.tensor_tensor(
-                out=gated[chunk][:], in0=gates[chunk][:], in1=states[chunk][:], op=ALU.mult
+                out=gated[(pair, chunk)][:], in0=gates[chunk][:], in1=states[chunk][:], op=ALU.mult
             )
 
-        def drive_and_sum(pair, chunk):
-            drive_bank = new_bank()
-            multiply(drive_bank[:], "W_B_c", chunk, ("c", pair), everything, start=True, stop=False)
-            multiply(drive_bank[:], "W_B_z", chunk, ("z", pair), everything, start=False, stop=True)
+        def drive_and_sum(pair, chunk, cols=everything):
+            if pair not in out_t:
+                out_t[pair] = work.tile([P, CHUNKS, PAIR], F32, name="out_t", bufs=3)
+            drive = new_bank()[:, 0 : cols.stop - cols.start]
+            multiply(drive, "W_B_c", chunk, ("c", pair), cols, start=True, stop=False)
+            multiply(drive, "W_B_z", chunk, ("z", pair), cols, start=False, stop=True)
             nc.vector.scalar_tensor_tensor(
-                out=out_t[pair][:, chunk, :],
-                in0=drive_bank[:],
+                out=out_t[pair][:, chunk, cols],
+                in0=drive,
                 scalar=vector_cols[:, PACK + chunk : PACK + chunk + 1],
-                in1=gated[chunk][:],
+                in1=gated[(pair, chunk)][:, cols],
                 op0=ALU.add,
                 op1=ALU.add,
             )
 
 
-        def transpose_out(slab):
+        def transpose_out(slab, e, copy):
             pair, half = divmod(slab, 2)
-            result = work.tile([P, 2 * WIDTH], F32, name="result")
-            for e in range(2):
-                cols = slice(half * SLAB + e * P, half * SLAB + (e + 1) * P)
-                bank = new_bank()
-                parts = bank[:].rearrange("q (t i) -> q t i", t=CHUNKS)
-                for chunk in range(CHUNKS):
-                    nc.tensor.transpose(parts[:, chunk, :], out_t[pair][:, chunk, cols], identity[:])
-                nc.scalar.copy(
-                    out=result[:, e * WIDTH : (e + 1) * WIDTH].rearrange(
-                        "q (u i e2) -> q u i e2", u=2, e2=2
-                    ),
-                    in_=bank[:].rearrange("q (u e2 i) -> q u i e2", u=2, e2=2),
-                )
-            nc.sync.dma_start(
-                out=out[slab * SLAB : (slab + 1) * SLAB, :].rearrange("(q e) d -> q (e d)", e=2),
-                in_=result[:],
+            if e == 0:
+                results[slab] = work.tile([P, 2 * WIDTH], F32, name="result", bufs=3)
+            result = results[slab]
+            cols = slice(half * SLAB + e * P, half * SLAB + (e + 1) * P)
+            bank = new_bank()
+            parts = bank[:].rearrange("q (t i) -> q t i", t=CHUNKS)
+            for chunk in range(CHUNKS):
+                nc.tensor.transpose(parts[:, chunk, :], out_t[pair][:, chunk, cols], identity[:])
+            copy(
+                out=result[:, e * WIDTH : (e + 1) * WIDTH].rearrange(
+                    "q (u i e2) -> q u i e2", u=2, e2=2
+                ),
+                in_=bank[:].rearrange("q (u e2 i) -> q u i e2", u=2, e2=2),
             )
+            if e == 1:
+                nc.sync.dma_start(
+                    out=out[slab * SLAB : (slab + 1) * SLAB, :].rearrange("(q e) d -> q (e d)", e=2),
+                    in_=result[:],
+                )
 
 
         identity = consts.tile([P, P], F32, name="identity")
@@ -261,66 +267,91 @@ def tile_wavesubsystem_pa_t_kernel(
                 out=vector_rows[2 * v : 2 * v + 2, :], in_=vector.rearrange("(u x) -> u x", u=2)
             )
 
-        load_slab(0)
+        load_slab(0, ("w",))
         load_k_first_weight("A_V")
-        load_slab(1)
+        load_slab(1, ("w",))
+        load_slab(0, ("c",))
         for half in range(2):
             rows[("A_U", half)] = consts.tile([P, 2 * WIDTH], BF16, name="rows_A_U_%d" % half)
             load_rows(rows[("A_U", half)], A_U, half)
+        load_slab(1, ("c",))
         load_k_first_weight("W_mod")
+        load_slab(0, ("z",))
+        load_slab(1, ("z",))
         load_slab(2)
         load_k_first_weight("W_B_c")
         load_k_first_weight("W_B_z")
         for slab in range(3, ROW_BUFS):
             load_slab(slab)
 
-        transpose_in(0)
-        quantise_k_first_weight("A_V")
-        for name in ("w", "c", "z"):
-            quantise_slab(name, 0)
-        transpose_in(1)
-        hidden(0)
-        for name in ("w", "c", "z"):
-            quantise_slab(name, 1)
-        quantise_a_u()
+        V, S = nc.vector.tensor_copy, nc.scalar.copy
+        transpose_in(0, ("w",), S)
+        for chunk, copy in enumerate((V, V, V, S)):
+            stage_chunk("A_V", chunk, copy)
+        transpose_in(1, ("w",), S)
+        quantise_slab("w", 0)
+        quantise_weight("A_V")
+        quantise_slab("w", 1)
+        for slab in range(2):
+            hidden(slab, 0, S)
+            hidden(slab, 1, V)
+        transpose_in(0, ("c",), S)
+        stage_a_u(0)
+        stage_a_u(1)
+        transpose_in(1, ("c",), S)
+        for chunk, copy in enumerate((V, V, V, S)):
+            stage_chunk("W_mod", chunk, copy)
         spread_vectors()
-        hidden(1)
+        transpose_in(0, ("z",), S)
+        transpose_in(1, ("z",), S)
         quantise_slab("h", 0)
-        quantise_k_first_weight("W_mod")
+        quantise_weight("A_U")
         quantise_slab("h", 1)
-        transpose_in(2)
-        quantise_k_first_weight("W_B_c")
-        quantise_k_first_weight("W_B_z")
+        quantise_weight("W_mod")
+        quantise_slab("c", 0)
+        quantise_slab("c", 1)
+        transpose_in(2, ("w", "c", "z"), S)
+        for name in ("W_B_c", "W_B_z"):
+            for chunk, copy in enumerate((V, V, S, S)):
+                stage_chunk(name, chunk, copy)
+        quantise_slab("z", 0)
+        quantise_slab("z", 1)
+        quantise_weight("W_B_c")
+        quantise_weight("W_B_z")
 
         for step in range(N_SLABS + OUT_LAG):
-            pair, half = divmod(step, 2)
-            chunk = 2 * half
-            last_pair, last_half = divmod(step - 1, 2)
-            last_chunk = 2 * last_half
+            coming = step + IN_LEAD < N_SLABS
+            fed = step + HIDDEN_LEAD < N_SLABS
             working = step < N_SLABS
-            summing = 0 < step <= N_SLABS
-            if step + IN_LEAD < N_SLABS:
-                transpose_in(step + IN_LEAD)
+            pair, half = divmod(step, 2)
+            first, second = 2 * half, 2 * half + 1
+            if 2 <= step + 1 < N_SLABS:
+                quantise_slab("h", step + 1)
+            if fed:
+                quantise_slab("w", step + HIDDEN_LEAD)
+            if working:
+                gate(pair, first)
+                gate(pair, second)
+            if fed:
+                quantise_slab("z", step + HIDDEN_LEAD)
+            if coming:
+                transpose_in(step + IN_LEAD, ("w", "c", "z"), S)
+            if working:
+                state(pair, first)
+                gate_the_state(pair, first)
+            if fed:
+                quantise_slab("c", step + HIDDEN_LEAD)
+            if working:
+                state(pair, second)
+                gate_the_state(pair, second)
             if step >= OUT_LAG:
-                transpose_out(step - OUT_LAG)
-            if step + HIDDEN_LEAD < N_SLABS:
-                for name in ("w", "c", "z"):
-                    quantise_slab(name, step + HIDDEN_LEAD)
-            if 0 < step and step - 1 + HIDDEN_LEAD < N_SLABS:
-                quantise_slab("h", step - 1 + HIDDEN_LEAD)
-            if summing:
-                gate_the_state(last_chunk + 1)
-                if last_half == 0:
-                    out_t[last_pair] = work.tile([P, CHUNKS, PAIR], F32, name="out_t")
-            if working:
-                gate(pair, chunk)
-                state(pair, chunk)
-                gate(pair, chunk + 1)
-                state(pair, chunk + 1)
-            if step + HIDDEN_LEAD < N_SLABS:
-                hidden(step + HIDDEN_LEAD)
-            if summing:
-                drive_and_sum(last_pair, last_chunk)
-                drive_and_sum(last_pair, last_chunk + 1)
-            if working:
-                gate_the_state(chunk)
+                transpose_out(step - OUT_LAG, 0, V)
+                transpose_out(step - OUT_LAG, 1, S)
+            if 0 < step <= N_SLABS:
+                last_pair, last_half = divmod(step - 1, 2)
+                drive_and_sum(last_pair, 2 * last_half)
+            if fed:
+                hidden(step + HIDDEN_LEAD, 0, S)
+                hidden(step + HIDDEN_LEAD, 1, S)
+            if 0 < step <= N_SLABS:
+                drive_and_sum(last_pair, 2 * last_half + 1)

@@ -22,7 +22,6 @@ PAIR = 2 * SLAB
 ROW_BUFS = 6
 IN_LEAD = 3
 HIDDEN_LEAD = 2
-OUT_LAG = 3
 
 FLOPS = 2 * ROWS * WIDTH * 5 * WIDTH
 
@@ -168,7 +167,6 @@ def tile_wavesubsystem_pa_t_kernel(
             nc.vector.tensor_copy(out=words[:], in_=bank[:, 0:8])
             nc.vector.tensor_copy(out=vector_cols[:], in_=words[:].bitcast(BF16))
             nc.scalar.activation(out=a_cols[:], in_=vector_cols[:, 8:12], func=ACT.Tanh)
-            nc.vector.tensor_scalar_mul(out=a_cols[:], in0=a_cols[:], scalar1=0.9)
 
 
         def hidden(slab, e, copy):
@@ -285,10 +283,21 @@ def tile_wavesubsystem_pa_t_kernel(
             load_slab(slab)
 
         V, S = nc.vector.tensor_copy, nc.scalar.copy
+        warm = consts.tile([P, WIDTH], BF16, name="warm")
+        nc.vector.memset(warm[:], 0.0)
+
+        def keep_warm(count):
+            bank = new_bank()
+            for turn in range(count):
+                nc.tensor.matmul(bank[:], lhsT=warm[:, 0:P], rhs=warm[:], start=True, stop=True)
+
+        keep_warm(4)
         transpose_in(0, ("w",), S)
         for chunk, copy in enumerate((V, V, V, S)):
             stage_chunk("A_V", chunk, copy)
+        keep_warm(1)
         transpose_in(1, ("w",), S)
+        keep_warm(2)
         quantise_slab("w", 0)
         quantise_weight("A_V")
         quantise_slab("w", 1)
@@ -299,27 +308,28 @@ def tile_wavesubsystem_pa_t_kernel(
         stage_a_u(0)
         stage_a_u(1)
         transpose_in(1, ("c",), S)
-        for chunk, copy in enumerate((V, V, V, S)):
+        for chunk, copy in enumerate((V, V, V, V)):
             stage_chunk("W_mod", chunk, copy)
         spread_vectors()
         transpose_in(0, ("z",), S)
         transpose_in(1, ("z",), S)
+        quantise_slab("c", 0)
+        quantise_slab("c", 1)
+        quantise_weight("W_mod")
         quantise_slab("h", 0)
         quantise_weight("A_U")
         quantise_slab("h", 1)
-        quantise_weight("W_mod")
-        quantise_slab("c", 0)
-        quantise_slab("c", 1)
+        nc.vector.tensor_scalar_mul(out=a_cols[:], in0=a_cols[:], scalar1=0.9)
         transpose_in(2, ("w", "c", "z"), S)
         for name in ("W_B_c", "W_B_z"):
-            for chunk, copy in enumerate((V, V, S, S)):
+            for chunk, copy in enumerate((V, V, V, S)):
                 stage_chunk(name, chunk, copy)
         quantise_slab("z", 0)
         quantise_slab("z", 1)
         quantise_weight("W_B_c")
         quantise_weight("W_B_z")
 
-        for step in range(N_SLABS + OUT_LAG):
+        for step in range(N_SLABS + 2):
             coming = step + IN_LEAD < N_SLABS
             fed = step + HIDDEN_LEAD < N_SLABS
             working = step < N_SLABS
@@ -344,9 +354,10 @@ def tile_wavesubsystem_pa_t_kernel(
             if working:
                 state(pair, second)
                 gate_the_state(pair, second)
-            if step >= OUT_LAG:
-                transpose_out(step - OUT_LAG, 0, V)
-                transpose_out(step - OUT_LAG, 1, S)
+            if half == 1 and pair > 0:
+                for slab in (2 * pair - 2, 2 * pair - 1):
+                    transpose_out(slab, 0, V)
+                    transpose_out(slab, 1, S)
             if 0 < step <= N_SLABS:
                 last_pair, last_half = divmod(step - 1, 2)
                 drive_and_sum(last_pair, 2 * last_half)

@@ -283,21 +283,10 @@ def tile_wavesubsystem_pa_t_kernel(
             load_slab(slab)
 
         V, S = nc.vector.tensor_copy, nc.scalar.copy
-        warm = consts.tile([P, WIDTH], BF16, name="warm")
-        nc.vector.memset(warm[:], 0.0)
-
-        def keep_warm(count):
-            bank = new_bank()
-            for turn in range(count):
-                nc.tensor.matmul(bank[:], lhsT=warm[:, 0:P], rhs=warm[:], start=True, stop=True)
-
-        keep_warm(4)
         transpose_in(0, ("w",), S)
         for chunk, copy in enumerate((V, V, V, S)):
             stage_chunk("A_V", chunk, copy)
-        keep_warm(1)
         transpose_in(1, ("w",), S)
-        keep_warm(2)
         quantise_slab("w", 0)
         quantise_weight("A_V")
         quantise_slab("w", 1)

from contextlib import ExitStack

import concourse.mybir as mybir
from concourse.masks import make_identity

F32 = mybir.dt.float32
BF16 = mybir.dt.bfloat16
U32 = mybir.dt.uint32
U8 = mybir.dt.uint8
FP8X4 = mybir.dt.float8_e4m3fn_x4
ALU = mybir.AluOpType
ACT = mybir.ActivationFunctionType

P = 128
PACK = 4
WIDTH = P * PACK
CHUNKS = WIDTH // P
ROWS = 4096
SLAB = 256
N_SLABS = ROWS // SLAB
PAIR = 2 * SLAB
ROW_BUFS = 6
IN_LEAD = 3
HIDDEN_LEAD = 2

FLOPS = 2 * ROWS * WIDTH * 5 * WIDTH


def tile_wavesubsystem_pa_t_kernel(
    tc, w_prev, z_t, c_t, A_diag, A_U, A_V, W_mod, b_mod, W_B, b_B, out
):
    nc = tc.nc
    activations = {"w": w_prev, "c": c_t, "z": z_t}
    k_first_weights = {
        "A_V": A_V,
        "W_mod": W_mod,
        "W_B_c": W_B[0:WIDTH, :],
        "W_B_z": W_B[WIDTH : 2 * WIDTH, :],
    }

    with ExitStack() as ctx:
        consts = ctx.enter_context(tc.tile_pool(name="consts", bufs=1))
        rows_pool = ctx.enter_context(tc.tile_pool(name="rows", bufs=ROW_BUFS))
        grouped_pool = ctx.enter_context(tc.tile_pool(name="grouped", bufs=3))
        staging = ctx.enter_context(tc.tile_pool(name="staging", bufs=3))
        codes_pool = ctx.enter_context(tc.tile_pool(name="codes", bufs=3))
        work = ctx.enter_context(tc.tile_pool(name="work", bufs=4))
        psum = ctx.enter_context(tc.psum_pool(name="psum", bufs=8))
        ctx.enter_context(tc.manual_schedule())

        def new_bank():
            return psum.tile([P, WIDTH], F32, name="bank", tag="bank")

        rows = {}
        grouped = {}
        codes = {}
        scales = {}
        staged = {}
        raw = {}
        gates = {}
        states = {}
        gated = {}
        results = {}
        out_t = {}

        def new_mx_operand(key, name):
            codes[key] = codes_pool.tile([P, WIDTH], U32, name=name + "_codes", align_bytes=64)
            scales[key] = codes_pool.tile([P, WIDTH], U8, name=name + "_scales", align_bytes=64)

        def quantise(source, key, first, count):
            nc.vector.quantize_mx(
                out=codes[key][:, first : first + count].bitcast(FP8X4),
                scales=scales[key][:, first : first + count],
                in_=source[:, PACK * first : PACK * (first + count)],
            )

        def multiply(acc, weight, chunk, moving, cols, start=True, stop=True):
            features = slice(chunk * P, (chunk + 1) * P)
            nc.tensor.matmul_mx(
                out=acc,
                lhsT=codes[weight][:, features].bitcast(FP8X4),
                lhsT_scale=scales[weight][:, features],
                rhs=codes[moving][:, cols].bitcast(FP8X4),
                rhs_scale=scales[moving][:, cols],
                start=start,
                stop=stop,
            )


        def load_rows(tile, source, slab):
            nc.sync.dma_start(
                out=tile[:],
                in_=source[slab * SLAB : (slab + 1) * SLAB, :].rearrange("(q e) k -> q (e k)", e=2),
            )

        def load_slab(slab, names=("w", "c", "z")):
            for name in names:
                rows[(name, slab)] = rows_pool.tile([P, 2 * WIDTH], BF16, name="rows_" + name)
                load_rows(rows[(name, slab)], activations[name], slab)

        def load_k_first_weight(name):
            raw[name] = consts.tile([P, PACK * WIDTH], BF16, name="raw_" + name)
            nc.sync.dma_start(
                out=raw[name][:].rearrange("i (u x) -> i u x", u=2),
                in_=k_first_weights[name].rearrange("(u i e) n -> i u (e n)", u=2, e=2),
            )


        def transpose_slab(tile, target, half, copy=nc.scalar.copy):
            words = tile[:].bitcast(F32).rearrange("q (e u i) -> q e u i", e=2, u=2)
            bank = new_bank()
            planes = bank[:].rearrange("i (u e q) -> i u e q", u=2, e=2)
            for e in range(2):
                for u in range(2):
                    nc.tensor.transpose(planes[:, u, e, :], words[:, e, u, :], identity[:])
            pairs = target[:].bitcast(F32).rearrange("i (col u) -> i col u", u=2)
            copy(
                out=pairs[:, half * SLAB : (half + 1) * SLAB, :],
                in_=bank[:].rearrange("i (u col) -> i col u", u=2),
            )

        def transpose_in(slab, names=("w", "c", "z"), copy=nc.scalar.copy):
            pair, half = divmod(slab, 2)
            for name in names:
                if (name, pair) not in grouped:
                    grouped[(name, pair)] = grouped_pool.tile(
                        [P, PACK * PAIR], BF16, name="grouped_" + name, align_bytes=64
                    )
                    new_mx_operand((name, pair), name)
                transpose_slab(rows[(name, slab)], grouped[(name, pair)], half, copy)
            if "z" in names and slab + ROW_BUFS < N_SLABS:
                load_slab(slab + ROW_BUFS)

        def quantise_pair(name, pair):
            quantise(grouped[(name, pair)], (name, pair), 0, PAIR)

        def quantise_slab(name, slab):
            pair, half = divmod(slab, 2)
            quantise(grouped[(name, pair)], (name, pair), half * SLAB, SLAB)


        def stage_chunk(name, chunk, copy):
            source = raw[name][:].rearrange("i (t u q e) -> i t u e q", t=PACK, u=2, e=2)
            if name not in staged:
                staged[name] = staging.tile([P, PACK * WIDTH], BF16, name="staged", align_bytes=64)
            target = staged[name][:].rearrange("i (c q t) -> i c q t", c=CHUNKS, t=PACK)
            u, e = divmod(chunk, 2)
            copy(out=target[:, chunk], in_=source[:, :, u, e, :].rearrange("i t q -> i q t"))

        def quantise_weight(name):
            new_weight_operand(name)
            quantise(staged[name], name, 0, WIDTH)

        def new_weight_operand(name):
            codes[name] = consts.tile([P, WIDTH], U32, name=name + "_codes", align_bytes=64)
            scales[name] = consts.tile([P, WIDTH], U8, name=name + "_scales", align_bytes=64)

        def stage_a_u(half, copy=nc.scalar.copy):
            if "A_U" not in staged:
                staged["A_U"] = staging.tile([P, PACK * WIDTH], BF16, name="staged", align_bytes=64)
            transpose_slab(rows[("A_U", half)], staged["A_U"], half, copy)

        def spread_vectors():
            bank = new_bank()
            nc.tensor.transpose(bank[:, 0:P], vector_rows[:].bitcast(F32), identity[:])
            words = consts.tile([P, 8], F32, name="vector_words")
            nc.vector.tensor_copy(out=words[:], in_=bank[:, 0:8])
            nc.vector.tensor_copy(out=vector_cols[:], in_=words[:].bitcast(BF16))
            nc.scalar.activation(out=a_cols[:], in_=vector_cols[:, 8:12], func=ACT.Tanh)


        def hidden(slab, e, copy):
            pair, half = divmod(slab, 2)
            if ("h", pair) not in grouped:
                grouped[("h", pair)] = grouped_pool.tile(
                    [P, PACK * PAIR], BF16, name="grouped_h", align_bytes=64
                )
                new_mx_operand(("h", pair), "h")
            target = grouped[("h", pair)][:].rearrange("i (col t) -> i col t", t=PACK)
            cols = slice(half * SLAB + e * P, half * SLAB + (e + 1) * P)
            bank = new_bank()
            parts = bank[:].rearrange("i (t q) -> i t q", t=PACK)
            for t in range(PACK):
                multiply(parts[:, t, :], "A_V", t, ("w", pair), cols)
            copy(out=target[:, cols, :], in_=parts.rearrange("i t q -> i q t"))


        everything = slice(0, PAIR)

        def gate(pair, chunk):
            gate_bank = new_bank()
            multiply(gate_bank[:], "W_mod", chunk, ("c", pair), everything)
            gates[chunk] = work.tile([P, PAIR], F32, name="gate")
            nc.scalar.activation(
                out=gates[chunk][:], in_=gate_bank[:], func=ACT.Tanh, bias=vector_cols[:, chunk : chunk + 1]
            )

        def state(pair, chunk):
            state_bank = new_bank()
            multiply(state_bank[:], "A_U", chunk, ("h", pair), everything)
            states[chunk] = work.tile([P, PAIR], F32, name="state")
            w_t = grouped[("w", pair)][:].rearrange("i (col t) -> i col t", t=PACK)[:, :, chunk]
            nc.vector.scalar_tensor_tensor(
                out=states[chunk][:],
                in0=w_t,
                scalar=a_cols[:, chunk : chunk + 1],
                in1=state_bank[:],
                op0=ALU.mult,
                op1=ALU.add,
            )

        def gate_the_state(pair, chunk, engine=nc.gpsimd):
            gated[(pair, chunk)] = work.tile([P, PAIR], F32, name="gated", bufs=6)
            engine.tensor_tensor(
                out=gated[(pair, chunk)][:], in0=gates[chunk][:], in1=states[chunk][:], op=ALU.mult
            )

        def drive_and_sum(pair, chunk, cols=everything):
            if pair not in out_t:
                out_t[pair] = work.tile([P, CHUNKS, PAIR], F32, name="out_t", bufs=3)
            drive = new_bank()[:, 0 : cols.stop - cols.start]
            multiply(drive, "W_B_c", chunk, ("c", pair), cols, start=True, stop=False)
            multiply(drive, "W_B_z", chunk, ("z", pair), cols, start=False, stop=True)
            nc.vector.scalar_tensor_tensor(
                out=out_t[pair][:, chunk, cols],
                in0=drive,
                scalar=vector_cols[:, PACK + chunk : PACK + chunk + 1],
                in1=gated[(pair, chunk)][:, cols],
                op0=ALU.add,
                op1=ALU.add,
            )


        def transpose_out(slab, e, copy):
            pair, half = divmod(slab, 2)
            if e == 0:
                results[slab] = work.tile([P, 2 * WIDTH], F32, name="result", bufs=3)
            result = results[slab]
            cols = slice(half * SLAB + e * P, half * SLAB + (e + 1) * P)
            bank = new_bank()
            parts = bank[:].rearrange("q (t i) -> q t i", t=CHUNKS)
            for chunk in range(CHUNKS):
                nc.tensor.transpose(parts[:, chunk, :], out_t[pair][:, chunk, cols], identity[:])
            copy(
                out=result[:, e * WIDTH : (e + 1) * WIDTH].rearrange(
                    "q (u i e2) -> q u i e2", u=2, e2=2
                ),
                in_=bank[:].rearrange("q (u e2 i) -> q u i e2", u=2, e2=2),
            )
            if e == 1:
                nc.sync.dma_start(
                    out=out[slab * SLAB : (slab + 1) * SLAB, :].rearrange("(q e) d -> q (e d)", e=2),
                    in_=result[:],
                )


        identity = consts.tile([P, P], F32, name="identity")
        make_identity(nc, identity[:])
        vector_rows = consts.tile([P, 2 * P], BF16, name="vector_rows")
        vector_cols = consts.tile([P, 16], F32, name="vector_cols")
        a_cols = consts.tile([P, CHUNKS], F32, name="a_cols")
        nc.vector.memset(vector_rows[:], 0.0)
        for v, vector in enumerate((b_mod, b_B, A_diag)):
            nc.scalar.dma_start(
                out=vector_rows[2 * v : 2 * v + 2, :], in_=vector.rearrange("(u x) -> u x", u=2)
            )

        load_slab(0, ("w",))
        load_k_first_weight("A_V")
        load_slab(1, ("w",))
        load_slab(0, ("c",))
        for half in range(2):
            rows[("A_U", half)] = consts.tile([P, 2 * WIDTH], BF16, name="rows_A_U_%d" % half)
            load_rows(rows[("A_U", half)], A_U, half)
        load_slab(1, ("c",))
        load_k_first_weight("W_mod")
        load_slab(0, ("z",))
        load_slab(1, ("z",))
        load_slab(2)
        load_k_first_weight("W_B_c")
        load_k_first_weight("W_B_z")
        for slab in range(3, ROW_BUFS):
            load_slab(slab)

        V, S = nc.vector.tensor_copy, nc.scalar.copy
        transpose_in(0, ("w",), S)
        for chunk, copy in enumerate((V, V, V, S)):
            stage_chunk("A_V", chunk, copy)
        transpose_in(1, ("w",), S)
        quantise_slab("w", 0)
        quantise_weight("A_V")
        quantise_slab("w", 1)
        for slab in range(2):
            hidden(slab, 0, S)
            hidden(slab, 1, V)
        transpose_in(0, ("c",), S)
        stage_a_u(0)
        stage_a_u(1)
        transpose_in(1, ("c",), S)
        for chunk, copy in enumerate((V, V, V, V)):
            stage_chunk("W_mod", chunk, copy)
        spread_vectors()
        transpose_in(0, ("z",), S)
        transpose_in(1, ("z",), S)
        quantise_slab("c", 0)
        quantise_slab("c", 1)
        quantise_weight("W_mod")
        quantise_slab("h", 0)
        quantise_weight("A_U")
        quantise_slab("h", 1)
        nc.vector.tensor_scalar_mul(out=a_cols[:], in0=a_cols[:], scalar1=0.9)
        transpose_in(2, ("w", "c", "z"), S)
        for name in ("W_B_c", "W_B_z"):
            for chunk, copy in enumerate((V, V, V, S)):
                stage_chunk(name, chunk, copy)
        quantise_slab("z", 0)
        quantise_slab("z", 1)
        quantise_weight("W_B_c")
        quantise_weight("W_B_z")

        for step in range(N_SLABS + 2):
            coming = step + IN_LEAD < N_SLABS
            fed = step + HIDDEN_LEAD < N_SLABS
            working = step < N_SLABS
            pair, half = divmod(step, 2)
            first, second = 2 * half, 2 * half + 1
            if 2 <= step + 1 < N_SLABS:
                quantise_slab("h", step + 1)
            if fed:
                quantise_slab("w", step + HIDDEN_LEAD)
            if working:
                gate(pair, first)
                gate(pair, second)
            if fed:
                quantise_slab("z", step + HIDDEN_LEAD)
            if coming:
                transpose_in(step + IN_LEAD, ("w", "c", "z"), S)
            if working:
                state(pair, first)
                gate_the_state(pair, first)
            if fed:
                quantise_slab("c", step + HIDDEN_LEAD)
            if working:
                state(pair, second)
                gate_the_state(pair, second)
            if half == 1 and pair > 0:
                for slab in (2 * pair - 2, 2 * pair - 1):
                    transpose_out(slab, 0, V)
                    transpose_out(slab, 1, S)
            if 0 < step <= N_SLABS:
                last_pair, last_half = divmod(step - 1, 2)
                drive_and_sum(last_pair, 2 * last_half)
            if fed:
                hidden(step + HIDDEN_LEAD, 0, S)
                hidden(step + HIDDEN_LEAD, 1, S)
            if 0 < step <= N_SLABS:
                drive_and_sum(last_pair, 2 * last_half + 1)
